import numpy as np
import ml_dtypes


def mxq(x, axis, fmt="e4m3"):
    dtype, down = {"e4m3": (ml_dtypes.float8_e4m3fn, 7), "e5m2": (ml_dtypes.float8_e5m2, 14)}[fmt]
    v = np.moveaxis(np.asarray(x, np.float32).astype(ml_dtypes.bfloat16).astype(np.float64), axis, -1)
    blocks = v.reshape(v.shape[:-1] + (-1, 32))
    amax = np.abs(blocks).max(-1, keepdims=True)
    byte = np.maximum(np.where(amax > 0, np.frexp(amax)[1] - 1 + 127, 0) - down, 1)
    scale = np.exp2(byte - 127.0)
    codes = (blocks / scale).astype(np.float32).astype(dtype).astype(np.float64)
    return np.moveaxis((codes * scale).reshape(v.shape), -1, axis)


WIDE = False


def mx_kscale(k):
    if not WIDE:
        return np.ones(k)
    levels = np.array([10, -10, 5, -5, 0])
    a = np.random.permutation(np.resize(levels, k // 512 * 4)).reshape(k // 512, 4)
    idx = np.arange(k)
    return np.exp2(a[idx // 512, idx % 128 // 32])


BF16 = ml_dtypes.bfloat16


def bf(x):
    return np.asarray(x, np.float32).astype(BF16)


def f64(x):
    return np.asarray(x).astype(np.float64)


E2M1 = np.array([0.0, 0.5, 1.0, 1.5, 2.0, 3.0, 4.0, 6.0, -0.0, -0.5, -1.0, -1.5, -2.0, -3.0, -4.0, -6.0])


def pack_weight(w, fmt):
    k, n = w.shape
    w = f64(bf(w)).reshape(k // 32, 32, n)
    amax = np.abs(w).max(1)
    if fmt == "e4m3":
        byte = np.frexp(amax)[1] - 1 + 127 - 7
    else:
        mant, ex = np.frexp(amax / 6.0)
        byte = np.where(mant > 0.5, ex, ex - 1) + 127
    byte = np.clip(np.where(amax > 0, byte, 1), 1, 254)
    scaled = (w * np.exp2(127.0 - byte)[:, None, :]).reshape(k, n).astype(np.float32)
    by_word = np.ascontiguousarray(scaled.reshape(k // 512, 128, 4, n).transpose(0, 1, 3, 2))
    if fmt == "e4m3":
        words = by_word.astype(ml_dtypes.float8_e4m3fn).view(np.uint8)
    else:
        c = by_word.astype(ml_dtypes.float4_e2m1fn).view(np.uint8) & 0xF
        words = c[..., 0::2] | (c[..., 1::2] << 4)
    return np.ascontiguousarray(words), np.ascontiguousarray(byte.astype(np.uint8).reshape(k // 512, 16, n))


def unpack_weight(words, scales, fmt):
    g, p, n, _ = words.shape
    if fmt == "e4m3":
        vals = np.ascontiguousarray(words).view(ml_dtypes.float8_e4m3fn).astype(np.float64)
    else:
        nib = np.empty((g, p, n, 4), np.uint8)
        nib[..., 0::2] = words & 0xF
        nib[..., 1::2] = words >> 4
        vals = E2M1[nib]
    vals = vals * np.repeat(np.exp2(scales.astype(np.float64) - 127.0), 8, axis=1)[..., None]
    return vals.transpose(0, 1, 3, 2).reshape(g * 512, n)

def pack4(w):
    words, scales = pack_weight(w, "e2m1")
    return words.reshape(words.shape[0], 128, -1), scales


def unpack4(words, scales):
    return unpack_weight(words.reshape(words.shape[0], 128, -1, 2), scales, "e2m1")


B, N, D, DO, H, HID = 12, 128, 512, 512, 8, 2048


def setup_inputs():
    s, t = mx_kscale(D), mx_kscale(D)
    adj = np.random.uniform(size=(N, N))
    adj = adj / adj.sum(-1, keepdims=True)
    h_norm = bf(np.random.standard_normal((B, N, D)) * s)
    o_attn = bf(np.random.standard_normal((B, N, D)) * 0.25 * t)
    a_gcn = bf(adj + np.random.standard_normal((N, N)) * 0.5 / np.sqrt(N))
    w_proj_words, w_proj_scales = pack4(np.random.standard_normal((D, DO)) * 2.0 / np.sqrt(D) / t[:, None])
    b_proj = bf(np.random.standard_normal(DO) * 0.1)
    gcn_w_words, gcn_w_scales = pack4(np.random.standard_normal((D, DO)) / np.sqrt(D) / s[:, None])
    gcn_m = bf(1.0 + 0.1 * np.random.standard_normal(DO))
    return {
        "h_norm": h_norm,
        "o_attn": o_attn,
        "a_gcn": a_gcn,
        "w_proj_words": w_proj_words,
        "w_proj_scales": w_proj_scales,
        "b_proj": b_proj,
        "gcn_w_words": gcn_w_words,
        "gcn_w_scales": gcn_w_scales,
        "gcn_m": gcn_m,
    }


def reference(h_norm, o_attn, a_gcn, w_proj_words, w_proj_scales, b_proj, gcn_w_words, gcn_w_scales, gcn_m):
    o = (mxq(f64(o_attn), 2, "e4m3") @ unpack4(w_proj_words, w_proj_scales)) + f64(b_proj)
    agg = f64(a_gcn) @ f64(h_norm)
    g = (mxq(agg, 2, "e4m3") @ unpack4(gcn_w_words, gcn_w_scales)) * f64(gcn_m)
    return o + g

@@ -1,0 +1,167 @@
+from contextlib import ExitStack
+
+import concourse.mybir as mybir
+from concourse.masks import make_identity
+
+F32 = mybir.dt.float32
+BF16 = mybir.dt.bfloat16
+I32 = mybir.dt.int32
+U32 = mybir.dt.uint32
+U8 = mybir.dt.uint8
+FP8X4 = mybir.dt.float8_e4m3fn_x4
+FP4X4 = mybir.dt.float4_e2m1fn_x4
+MULT = mybir.AluOpType.mult
+ADD = mybir.AluOpType.add
+
+P = 128
+PACK = 4
+SAMPLES = 12
+D = 512
+D_OUT = 512
+LOAD_SAMPLES = 2
+
+FLOPS = 2 * 2 * SAMPLES * P * D * D_OUT + 2 * SAMPLES * P * P * D
+
+
+def load_weight(nc, words_dram, scales_dram, words, plane):
+    nc.sync.dma_start(out=words.bitcast(I32), in_=words_dram[0].bitcast(I32))
+    for r in range(4):
+        nc.sync.dma_start(
+            out=plane[r:P:32, :].bitcast(I32), in_=scales_dram[0, r:16:4, :].bitcast(I32)
+        )
+
+
+def tile_gatblock_pa_kernel(
+    tc,
+    h_norm,
+    o_attn,
+    a_gcn,
+    w_proj_words,
+    w_proj_scales,
+    b_proj,
+    gcn_w_words,
+    gcn_w_scales,
+    gcn_m,
+    out,
+):
+    nc = tc.nc
+    with ExitStack() as pools:
+        const = pools.enter_context(tc.tile_pool(name="const", bufs=1))
+        stage = pools.enter_context(tc.tile_pool(name="stage", bufs=3))
+        psum = pools.enter_context(tc.psum_pool(name="psum", bufs=2))
+
+        w_planes = const.tile([P, 2, D_OUT], U8, align_bytes=64)
+        nc.vector.memset(w_planes[:].bitcast(I32), 0)
+        vec_rows = const.tile([P, 2, D_OUT], BF16)
+        nc.vector.memset(vec_rows[:], 0.0)
+        ones = const.tile([P, P], BF16)
+        nc.vector.memset(ones[:], 1.0)
+        ident_f32 = const.tile([P, P], F32)
+        make_identity(nc, ident_f32[:])
+        ident_bf16 = const.tile([P, P], BF16)
+        nc.vector.tensor_copy(out=ident_bf16[:], in_=ident_f32[:])
+
+        a_sb = const.tile([P, P], BF16)
+        gcn_words = const.tile([P, 2 * D_OUT], U8, align_bytes=64)
+        proj_words = const.tile([P, 2 * D_OUT], U8, align_bytes=64)
+        h_tiles = []
+        o_tiles = []
+        nc.sync.dma_start(out=a_sb[:], in_=a_gcn)
+        for c in range(SAMPLES // LOAD_SAMPLES):
+            rows = slice(c * LOAD_SAMPLES, (c + 1) * LOAD_SAMPLES)
+            h_sb = const.tile([P, LOAD_SAMPLES, D], BF16, name="h_sb%d" % c)
+            nc.sync.dma_start(out=h_sb[:], in_=h_norm[rows].rearrange("b n d -> n b d"))
+            h_tiles.append(h_sb)
+            if c == 0:
+                load_weight(nc, gcn_w_words, gcn_w_scales, gcn_words[:], w_planes[:, 0, :])
+            o_sb = const.tile([P, LOAD_SAMPLES, D], BF16, name="o_sb%d" % c)
+            nc.sync.dma_start(out=o_sb[:], in_=o_attn[rows].rearrange("b n d -> n b d"))
+            o_tiles.append(o_sb)
+            if c == 0:
+                load_weight(nc, w_proj_words, w_proj_scales, proj_words[:], w_planes[:, 1, :])
+                nc.sync.dma_start(out=vec_rows[0:1, 0, :], in_=gcn_m.unsqueeze(0))
+                nc.sync.dma_start(out=vec_rows[0:1, 1, :], in_=b_proj.unsqueeze(0))
+
+        aT_ps = psum.tile([P, P], BF16, tag="xt")
+        nc.tensor.transpose(aT_ps[:], a_sb[:], ident_bf16[:])
+        aT_sb = const.tile([P, P], BF16)
+        nc.vector.tensor_copy(out=aT_sb[:], in_=aT_ps[:])
+
+        m_ps = psum.tile([P, D_OUT], F32, tag="g")
+        nc.tensor.matmul(out=m_ps[:], lhsT=ones[:], rhs=vec_rows[:, 0, :], start=True, stop=True)
+        m_all = const.tile([P, D_OUT], F32)
+        nc.vector.tensor_copy(out=m_all[:], in_=m_ps[:])
+        b_ps = psum.tile([P, D_OUT], F32, tag="o")
+        nc.tensor.matmul(out=b_ps[:], lhsT=ones[:], rhs=vec_rows[:, 1, :], start=True, stop=True)
+        b_all = const.tile([P, D_OUT], F32)
+        nc.vector.tensor_copy(out=b_all[:], in_=b_ps[:])
+
+        agg_codes = const.tile([P, SAMPLES, P], U32, align_bytes=64)
+        agg_scales = const.tile([P, SAMPLES, P], U8, align_bytes=64)
+        o_codes = const.tile([P, SAMPLES, P], U32, align_bytes=64)
+        o_scales = const.tile([P, SAMPLES, P], U8, align_bytes=64)
+
+        def quantise_agg(b):
+            h = h_tiles[b // LOAD_SAMPLES][:, b % LOAD_SAMPLES, :]
+            agg_ps = psum.tile([P, PACK, P], F32, tag="agg")
+            for t in range(PACK):
+                nc.tensor.matmul(
+                    out=agg_ps[:, t, :], lhsT=h[:, t:D:PACK], rhs=aT_sb[:], start=True, stop=True
+                )
+            agg_grouped = stage.tile([P, P, PACK], BF16, align_bytes=64)
+            nc.scalar.copy(out=agg_grouped[:], in_=agg_ps[:].rearrange("p t i -> p i t"))
+            nc.vector.quantize_mx(
+                out=agg_codes[:, b, :].bitcast(FP8X4),
+                scales=agg_scales[:, b, :],
+                in_=agg_grouped[:].rearrange("p i t -> p (i t)"),
+            )
+
+        def quantise_o(b):
+            words = o_tiles[b // LOAD_SAMPLES][:, b % LOAD_SAMPLES, :].bitcast(F32)
+            xt_ps = psum.tile([P, 2, P], F32, tag="xt")
+            for u in range(2):
+                nc.tensor.transpose(xt_ps[:, u, :], words[:, u : D // 2 : 2], ident_f32[:])
+            o_grouped = stage.tile([P, P, PACK], BF16, align_bytes=64)
+            nc.scalar.copy(out=o_grouped[:].bitcast(F32), in_=xt_ps[:].rearrange("p u i -> p i u"))
+            nc.vector.quantize_mx(
+                out=o_codes[:, b, :].bitcast(FP8X4),
+                scales=o_scales[:, b, :],
+                in_=o_grouped[:].rearrange("p i t -> p (i t)"),
+            )
+
+        def finish(b):
+            g_ps = psum.tile([P, D_OUT], F32, tag="g")
+            nc.tensor.matmul_mx(
+                out=g_ps[:],
+                lhsT=agg_codes[:, b, :].bitcast(FP8X4),
+                lhsT_scale=agg_scales[:, b, :],
+                rhs=gcn_words[:].bitcast(FP4X4),
+                rhs_scale=w_planes[:, 0, :],
+                start=True,
+                stop=True,
+            )
+            o_ps = psum.tile([P, D_OUT], F32, tag="o")
+            nc.tensor.matmul_mx(
+                out=o_ps[:],
+                lhsT=o_codes[:, b, :].bitcast(FP8X4),
+                lhsT_scale=o_scales[:, b, :],
+                rhs=proj_words[:].bitcast(FP4X4),
+                rhs_scale=w_planes[:, 1, :],
+                start=True,
+                stop=True,
+            )
+            scaled = stage.tile([P, D_OUT], F32)
+            nc.vector.tensor_tensor(out=scaled[:], in0=g_ps[:], in1=m_all[:], op=MULT)
+            summed = stage.tile([P, D_OUT], F32)
+            nc.vector.tensor_tensor(out=summed[:], in0=o_ps[:], in1=scaled[:], op=ADD)
+            result = stage.tile([P, D_OUT], F32)
+            nc.gpsimd.tensor_tensor(out=result[:], in0=summed[:], in1=b_all[:], op=ADD)
+            nc.sync.dma_start(out=out[b], in_=result[:])
+
+        quantise_agg(0)
+        quantise_o(0)
+        for b in range(SAMPLES):
+            if b + 1 < SAMPLES:
+                quantise_agg(b + 1)
+                quantise_o(b + 1)
+            finish(b)

@@ -18,7 +18,9 @@ PACK = 4
 SAMPLES = 12
 D = 512
 D_OUT = 512
-LOAD_SAMPLES = 2
+PAIR = 2
+LEAD = 3
+RUNS = ((0, 2), (2, 2), (4, 4), (8, 4))
 
 FLOPS = 2 * 2 * SAMPLES * P * D * D_OUT + 2 * SAMPLES * P * P * D
 
@@ -47,8 +49,9 @@ def tile_gatblock_pa_kernel(
     nc = tc.nc
     with ExitStack() as pools:
         const = pools.enter_context(tc.tile_pool(name="const", bufs=1))
-        stage = pools.enter_context(tc.tile_pool(name="stage", bufs=3))
+        stage = pools.enter_context(tc.tile_pool(name="stage", bufs=4))
         psum = pools.enter_context(tc.psum_pool(name="psum", bufs=2))
+        pools.enter_context(tc.manual_schedule())
 
         w_planes = const.tile([P, 2, D_OUT], U8, align_bytes=64)
         nc.vector.memset(w_planes[:].bitcast(I32), 0)
@@ -56,90 +59,126 @@ def tile_gatblock_pa_kernel(
         nc.vector.memset(vec_rows[:], 0.0)
         ones = const.tile([P, P], BF16)
         nc.vector.memset(ones[:], 1.0)
+        ident_bf16 = const.tile([P, P], BF16)
+        make_identity(nc, ident_bf16[:])
         ident_f32 = const.tile([P, P], F32)
         make_identity(nc, ident_f32[:])
-        ident_bf16 = const.tile([P, P], BF16)
-        nc.vector.tensor_copy(out=ident_bf16[:], in_=ident_f32[:])
 
+        nc.scalar.dma_start(out=vec_rows[0:1, 1, :], in_=b_proj.unsqueeze(0))
+        nc.scalar.dma_start(out=vec_rows[0:1, 0, :], in_=gcn_m.unsqueeze(0))
         a_sb = const.tile([P, P], BF16)
         gcn_words = const.tile([P, 2 * D_OUT], U8, align_bytes=64)
         proj_words = const.tile([P, 2 * D_OUT], U8, align_bytes=64)
         h_tiles = []
-        o_tiles = []
-        nc.sync.dma_start(out=a_sb[:], in_=a_gcn)
-        for c in range(SAMPLES // LOAD_SAMPLES):
-            rows = slice(c * LOAD_SAMPLES, (c + 1) * LOAD_SAMPLES)
-            h_sb = const.tile([P, LOAD_SAMPLES, D], BF16, name="h_sb%d" % c)
-            nc.sync.dma_start(out=h_sb[:], in_=h_norm[rows].rearrange("b n d -> n b d"))
+        for c in range(SAMPLES // PAIR):
+            h_sb = const.tile([P, PAIR, D], BF16, name="h_sb%d" % c)
             h_tiles.append(h_sb)
-            if c == 0:
-                load_weight(nc, gcn_w_words, gcn_w_scales, gcn_words[:], w_planes[:, 0, :])
-            o_sb = const.tile([P, LOAD_SAMPLES, D], BF16, name="o_sb%d" % c)
-            nc.sync.dma_start(out=o_sb[:], in_=o_attn[rows].rearrange("b n d -> n b d"))
+        o_tiles = []
+        for first, count in RUNS:
+            o_sb = const.tile([P, count, D], BF16, name="o_sb%d" % first)
             o_tiles.append(o_sb)
-            if c == 0:
-                load_weight(nc, w_proj_words, w_proj_scales, proj_words[:], w_planes[:, 1, :])
-                nc.sync.dma_start(out=vec_rows[0:1, 0, :], in_=gcn_m.unsqueeze(0))
-                nc.sync.dma_start(out=vec_rows[0:1, 1, :], in_=b_proj.unsqueeze(0))
+
+        def load_h(c):
+            rows = slice(c * PAIR, (c + 1) * PAIR)
+            nc.sync.dma_start(out=h_tiles[c][:], in_=h_norm[rows].rearrange("b n d -> n b d"))
+
+        def load_o(r):
+            first, count = RUNS[r]
+            nc.sync.dma_start(
+                out=o_tiles[r][:], in_=o_attn[first : first + count].rearrange("b n d -> n b d")
+            )
+
+        nc.sync.dma_start(out=a_sb[:], in_=a_gcn)
+        load_o(0)
+        load_h(0)
+        load_o(1)
+        load_weight(nc, w_proj_words, w_proj_scales, proj_words[:], w_planes[:, 1, :])
+        load_weight(nc, gcn_w_words, gcn_w_scales, gcn_words[:], w_planes[:, 0, :])
+        load_h(1)
+        load_h(2)
+        load_o(2)
+        load_h(3)
+        load_h(4)
+        load_o(3)
+        load_h(5)
 
         aT_ps = psum.tile([P, P], BF16, tag="xt")
         nc.tensor.transpose(aT_ps[:], a_sb[:], ident_bf16[:])
         aT_sb = const.tile([P, P], BF16)
         nc.vector.tensor_copy(out=aT_sb[:], in_=aT_ps[:])
-
-        m_ps = psum.tile([P, D_OUT], F32, tag="g")
-        nc.tensor.matmul(out=m_ps[:], lhsT=ones[:], rhs=vec_rows[:, 0, :], start=True, stop=True)
-        m_all = const.tile([P, D_OUT], F32)
-        nc.vector.tensor_copy(out=m_all[:], in_=m_ps[:])
         b_ps = psum.tile([P, D_OUT], F32, tag="o")
         nc.tensor.matmul(out=b_ps[:], lhsT=ones[:], rhs=vec_rows[:, 1, :], start=True, stop=True)
         b_all = const.tile([P, D_OUT], F32)
         nc.vector.tensor_copy(out=b_all[:], in_=b_ps[:])
+        m_ps = psum.tile([P, D_OUT], F32, tag="g")
+        nc.tensor.matmul(out=m_ps[:], lhsT=ones[:], rhs=vec_rows[:, 0, :], start=True, stop=True)
+        m_all = const.tile([P, D_OUT], F32)
+        nc.vector.tensor_copy(out=m_all[:], in_=m_ps[:])
 
         agg_codes = const.tile([P, SAMPLES, P], U32, align_bytes=64)
         agg_scales = const.tile([P, SAMPLES, P], U8, align_bytes=64)
         o_codes = const.tile([P, SAMPLES, P], U32, align_bytes=64)
         o_scales = const.tile([P, SAMPLES, P], U8, align_bytes=64)
+        agg_grouped = {}
+        o_grouped = {}
+        banks = {}
+        parts = {}
 
-        def quantise_agg(b):
-            h = h_tiles[b // LOAD_SAMPLES][:, b % LOAD_SAMPLES, :]
+        def transpose_run(r):
+            first, count = RUNS[r]
+            grouped = stage.tile([P, count, P, PACK], BF16, tag="o_grouped", bufs=2, align_bytes=64)
+            o_grouped[r] = grouped
+            xts = []
+            for q in range(count // PAIR):
+                xt_ps = psum.tile([P, PAIR, 2, P], F32, tag="xt")
+                xts.append(xt_ps)
+                for j in range(PAIR):
+                    words = o_tiles[r][:, q * PAIR + j, :].bitcast(F32)
+                    for u in range(2):
+                        nc.tensor.transpose(
+                            xt_ps[:, j, u, :], words[:, u : D // 2 : 2], ident_f32[:]
+                        )
+            return xts
+
+        def copy_run(r, xts):
+            for q in range(len(xts)):
+                nc.scalar.copy(
+                    out=o_grouped[r][:, q * PAIR : (q + 1) * PAIR, :, :].bitcast(F32),
+                    in_=xts[q][:].rearrange("p j u i -> p j i u"),
+                )
+
+        def quantise_run(r):
+            first, count = RUNS[r]
+            nc.vector.quantize_mx(
+                out=o_codes[:, first : first + count, :].rearrange("p b i -> p (b i)").bitcast(FP8X4),
+                scales=o_scales[:, first : first + count, :].rearrange("p b i -> p (b i)"),
+                in_=o_grouped[r][:].rearrange("p b i t -> p (b i t)"),
+            )
+
+        def mix(b, run):
+            h = h_tiles[b // PAIR][:, b % PAIR, :]
             agg_ps = psum.tile([P, PACK, P], F32, tag="agg")
+            xts = []
             for t in range(PACK):
+                if t == PACK // 2 and run is not None:
+                    xts = transpose_run(run)
                 nc.tensor.matmul(
                     out=agg_ps[:, t, :], lhsT=h[:, t:D:PACK], rhs=aT_sb[:], start=True, stop=True
                 )
-            agg_grouped = stage.tile([P, P, PACK], BF16, align_bytes=64)
-            nc.scalar.copy(out=agg_grouped[:], in_=agg_ps[:].rearrange("p t i -> p i t"))
+            if run is not None:
+                copy_run(run, xts)
+            grouped = stage.tile([P, P, PACK], BF16, tag="agg_grouped", align_bytes=64)
+            agg_grouped[b] = grouped
+            nc.scalar.copy(out=grouped[:], in_=agg_ps[:].rearrange("p t i -> p i t"))
+
+        def quantise_agg(b):
             nc.vector.quantize_mx(
                 out=agg_codes[:, b, :].bitcast(FP8X4),
                 scales=agg_scales[:, b, :],
-                in_=agg_grouped[:].rearrange("p i t -> p (i t)"),
+                in_=agg_grouped[b][:].rearrange("p i t -> p (i t)"),
             )
 
-        def quantise_o(b):
-            words = o_tiles[b // LOAD_SAMPLES][:, b % LOAD_SAMPLES, :].bitcast(F32)
-            xt_ps = psum.tile([P, 2, P], F32, tag="xt")
-            for u in range(2):
-                nc.tensor.transpose(xt_ps[:, u, :], words[:, u : D // 2 : 2], ident_f32[:])
-            o_grouped = stage.tile([P, P, PACK], BF16, align_bytes=64)
-            nc.scalar.copy(out=o_grouped[:].bitcast(F32), in_=xt_ps[:].rearrange("p u i -> p i u"))
-            nc.vector.quantize_mx(
-                out=o_codes[:, b, :].bitcast(FP8X4),
-                scales=o_scales[:, b, :],
-                in_=o_grouped[:].rearrange("p i t -> p (i t)"),
-            )
-
-        def finish(b):
-            g_ps = psum.tile([P, D_OUT], F32, tag="g")
-            nc.tensor.matmul_mx(
-                out=g_ps[:],
-                lhsT=agg_codes[:, b, :].bitcast(FP8X4),
-                lhsT_scale=agg_scales[:, b, :],
-                rhs=gcn_words[:].bitcast(FP4X4),
-                rhs_scale=w_planes[:, 0, :],
-                start=True,
-                stop=True,
-            )
+        def products(b):
             o_ps = psum.tile([P, D_OUT], F32, tag="o")
             nc.tensor.matmul_mx(
                 out=o_ps[:],
@@ -150,18 +189,71 @@ def tile_gatblock_pa_kernel(
                 start=True,
                 stop=True,
             )
-            scaled = stage.tile([P, D_OUT], F32)
-            nc.vector.tensor_tensor(out=scaled[:], in0=g_ps[:], in1=m_all[:], op=MULT)
-            summed = stage.tile([P, D_OUT], F32)
-            nc.vector.tensor_tensor(out=summed[:], in0=o_ps[:], in1=scaled[:], op=ADD)
-            result = stage.tile([P, D_OUT], F32)
-            nc.gpsimd.tensor_tensor(out=result[:], in0=summed[:], in1=b_all[:], op=ADD)
-            nc.sync.dma_start(out=out[b], in_=result[:])
+            g_ps = psum.tile([P, D_OUT], F32, tag="g")
+            nc.tensor.matmul_mx(
+                out=g_ps[:],
+                lhsT=agg_codes[:, b, :].bitcast(FP8X4),
+                lhsT_scale=agg_scales[:, b, :],
+                rhs=gcn_words[:].bitcast(FP4X4),
+                rhs_scale=w_planes[:, 0, :],
+                start=True,
+                stop=True,
+            )
+            banks[b] = (o_ps, g_ps)
 
+        def empty_banks(b, pieces):
+            o_ps, g_ps = banks[b]
+            biased = stage.tile([P, D_OUT], F32, tag="biased")
+            nc.vector.tensor_tensor(out=biased[:], in0=o_ps[:], in1=b_all[:], op=ADD)
+            scaled = stage.tile([P, D_OUT], F32, tag="scaled")
+            width = D_OUT // pieces
+            for c in range(pieces):
+                cols = slice(c * width, (c + 1) * width)
+                nc.vector.tensor_tensor(
+                    out=scaled[:, cols], in0=g_ps[:, cols], in1=m_all[:, cols], op=MULT
+                )
+            parts[b] = (biased, scaled)
+
+        def finish(b, engine, pieces):
+            biased, scaled = parts[b]
+            result = stage.tile([P, D_OUT], F32, tag="result")
+            width = D_OUT // pieces
+            for c in range(pieces):
+                cols = slice(c * width, (c + 1) * width)
+                engine.tensor_tensor(
+                    out=result[:, cols], in0=biased[:, cols], in1=scaled[:, cols], op=ADD
+                )
+                nc.sync.dma_start(out=out[b][:, cols], in_=result[:, cols])
+
+        run_of_first = {}
+        for r in range(2, len(RUNS)):
+            run_of_first[RUNS[r][0]] = r
+
+        copy_run(0, transpose_run(0))
+        quantise_run(0)
+        mix(0, None)
         quantise_agg(0)
-        quantise_o(0)
-        for b in range(SAMPLES):
-            if b + 1 < SAMPLES:
-                quantise_agg(b + 1)
-                quantise_o(b + 1)
-            finish(b)
+        mix(1, None)
+        copy_run(1, transpose_run(1))
+        pending_run = 1
+
+        for s in range(SAMPLES):
+            products(s)
+            woven = None
+            for b in range(PAIR, SAMPLES):
+                if max(b - LEAD, b // PAIR - 1) == s:
+                    mix(b, run_of_first.get(b))
+                    if b in run_of_first:
+                        woven = run_of_first[b]
+            last = s == SAMPLES - 1
+            empty_banks(s, 2 if last else 1)
+            for b in range(1, SAMPLES):
+                if max(b - 2, 0) == s:
+                    quantise_agg(b)
+            if pending_run is not None:
+                quantise_run(pending_run)
+            pending_run = woven
+            if last:
+                finish(s, nc.vector, 2)
+            else:
+                finish(s, nc.gpsimd, 1)

@@ -20,17 +20,17 @@ D = 512
 D_OUT = 512
 PAIR = 2
 LEAD = 3
-RUNS = ((0, 2), (2, 2), (4, 4), (8, 4))
+RUNS = ((0, 2), (2, 2), (4, 2), (6, 2), (8, 4))
 
 FLOPS = 2 * 2 * SAMPLES * P * D * D_OUT + 2 * SAMPLES * P * P * D
 
 
-def load_weight(nc, words_dram, scales_dram, words, plane):
+def load_words(nc, words_dram, words):
     nc.sync.dma_start(out=words.bitcast(I32), in_=words_dram[0].bitcast(I32))
-    for r in range(4):
-        nc.sync.dma_start(
-            out=plane[r:P:32, :].bitcast(I32), in_=scales_dram[0, r:16:4, :].bitcast(I32)
-        )
+
+
+def load_scales(nc, scales_dram, plane, r):
+    nc.sync.dma_start(out=plane[r:P:32, :].bitcast(I32), in_=scales_dram[0, r:16:4, :].bitcast(I32))
 
 
 def tile_gatblock_pa_kernel(
@@ -53,19 +53,20 @@ def tile_gatblock_pa_kernel(
         psum = pools.enter_context(tc.psum_pool(name="psum", bufs=2))
         pools.enter_context(tc.manual_schedule())
 
-        w_planes = const.tile([P, 2, D_OUT], U8, align_bytes=64)
-        nc.vector.memset(w_planes[:].bitcast(I32), 0)
         vec_rows = const.tile([P, 2, D_OUT], BF16)
         nc.vector.memset(vec_rows[:], 0.0)
+        w_planes = const.tile([P, 2, D_OUT], U8, align_bytes=64)
+        nc.vector.memset(w_planes[:].bitcast(I32), 0)
         ones = const.tile([P, P], BF16)
         nc.vector.memset(ones[:], 1.0)
+        warm = const.tile([P, 2], F32)
+        nc.gpsimd.memset(warm[:, 0:1], 0.0)
+        nc.scalar.copy(out=warm[:, 1:2], in_=warm[:, 0:1])
         ident_bf16 = const.tile([P, P], BF16)
         make_identity(nc, ident_bf16[:])
         ident_f32 = const.tile([P, P], F32)
         make_identity(nc, ident_f32[:])
 
-        nc.scalar.dma_start(out=vec_rows[0:1, 1, :], in_=b_proj.unsqueeze(0))
-        nc.scalar.dma_start(out=vec_rows[0:1, 0, :], in_=gcn_m.unsqueeze(0))
         a_sb = const.tile([P, P], BF16)
         gcn_words = const.tile([P, 2 * D_OUT], U8, align_bytes=64)
         proj_words = const.tile([P, 2 * D_OUT], U8, align_bytes=64)
@@ -91,29 +92,34 @@ def tile_gatblock_pa_kernel(
         nc.sync.dma_start(out=a_sb[:], in_=a_gcn)
         load_o(0)
         load_h(0)
+        nc.sync.dma_start(out=vec_rows[0:1, 1, :], in_=b_proj.unsqueeze(0))
+        load_words(nc, w_proj_words, proj_words[:])
+        for r in range(3):
+            load_scales(nc, w_proj_scales, w_planes[:, 1, :], r)
+        load_scales(nc, w_proj_scales, w_planes[:, 1, :], 3)
+        nc.sync.dma_start(out=vec_rows[0:1, 0, :], in_=gcn_m.unsqueeze(0))
+        load_words(nc, gcn_w_words, gcn_words[:])
+        for r in range(4):
+            load_scales(nc, gcn_w_scales, w_planes[:, 0, :], r)
         load_o(1)
-        load_weight(nc, w_proj_words, w_proj_scales, proj_words[:], w_planes[:, 1, :])
-        load_weight(nc, gcn_w_words, gcn_w_scales, gcn_words[:], w_planes[:, 0, :])
         load_h(1)
-        load_h(2)
         load_o(2)
-        load_h(3)
-        load_h(4)
+        load_h(2)
         load_o(3)
+        load_h(3)
+        load_o(4)
+        load_h(4)
         load_h(5)
 
         aT_ps = psum.tile([P, P], BF16, tag="xt")
         nc.tensor.transpose(aT_ps[:], a_sb[:], ident_bf16[:])
         aT_sb = const.tile([P, P], BF16)
         nc.vector.tensor_copy(out=aT_sb[:], in_=aT_ps[:])
-        b_ps = psum.tile([P, D_OUT], F32, tag="o")
+        b_ps = psum.tile([P, D_OUT], F32, tag="g")
         nc.tensor.matmul(out=b_ps[:], lhsT=ones[:], rhs=vec_rows[:, 1, :], start=True, stop=True)
         b_all = const.tile([P, D_OUT], F32)
         nc.vector.tensor_copy(out=b_all[:], in_=b_ps[:])
-        m_ps = psum.tile([P, D_OUT], F32, tag="g")
-        nc.tensor.matmul(out=m_ps[:], lhsT=ones[:], rhs=vec_rows[:, 0, :], start=True, stop=True)
         m_all = const.tile([P, D_OUT], F32)
-        nc.vector.tensor_copy(out=m_all[:], in_=m_ps[:])
 
         agg_codes = const.tile([P, SAMPLES, P], U32, align_bytes=64)
         agg_scales = const.tile([P, SAMPLES, P], U8, align_bytes=64)
@@ -121,8 +127,6 @@ def tile_gatblock_pa_kernel(
         o_scales = const.tile([P, SAMPLES, P], U8, align_bytes=64)
         agg_grouped = {}
         o_grouped = {}
-        banks = {}
-        parts = {}
 
         def transpose_run(r):
             first, count = RUNS[r]
@@ -142,7 +146,8 @@ def tile_gatblock_pa_kernel(
 
         def copy_run(r, xts):
             for q in range(len(xts)):
-                nc.scalar.copy(
+                copy = nc.vector.tensor_copy if r == 0 else nc.scalar.copy
+                copy(
                     out=o_grouped[r][:, q * PAIR : (q + 1) * PAIR, :, :].bitcast(F32),
                     in_=xts[q][:].rearrange("p j u i -> p j i u"),
                 )
@@ -178,7 +183,7 @@ def tile_gatblock_pa_kernel(
                 in_=agg_grouped[b][:].rearrange("p i t -> p (i t)"),
             )
 
-        def products(b):
+        def product_o(b):
             o_ps = psum.tile([P, D_OUT], F32, tag="o")
             nc.tensor.matmul_mx(
                 out=o_ps[:],
@@ -189,6 +194,9 @@ def tile_gatblock_pa_kernel(
                 start=True,
                 stop=True,
             )
+            return o_ps
+
+        def product_g(b):
             g_ps = psum.tile([P, D_OUT], F32, tag="g")
             nc.tensor.matmul_mx(
                 out=g_ps[:],
@@ -199,12 +207,14 @@ def tile_gatblock_pa_kernel(
                 start=True,
                 stop=True,
             )
-            banks[b] = (o_ps, g_ps)
+            return g_ps
 
-        def empty_banks(b, pieces):
-            o_ps, g_ps = banks[b]
+        def add_bias(o_ps):
             biased = stage.tile([P, D_OUT], F32, tag="biased")
             nc.vector.tensor_tensor(out=biased[:], in0=o_ps[:], in1=b_all[:], op=ADD)
+            return biased
+
+        def scale_g(g_ps, pieces):
             scaled = stage.tile([P, D_OUT], F32, tag="scaled")
             width = D_OUT // pieces
             for c in range(pieces):
@@ -212,10 +222,9 @@ def tile_gatblock_pa_kernel(
                 nc.vector.tensor_tensor(
                     out=scaled[:, cols], in0=g_ps[:, cols], in1=m_all[:, cols], op=MULT
                 )
-            parts[b] = (biased, scaled)
+            return scaled
 
-        def finish(b, engine, pieces):
-            biased, scaled = parts[b]
+        def finish(b, biased, scaled, engine, pieces):
             result = stage.tile([P, D_OUT], F32, tag="result")
             width = D_OUT // pieces
             for c in range(pieces):
@@ -224,6 +233,9 @@ def tile_gatblock_pa_kernel(
                     out=result[:, cols], in0=biased[:, cols], in1=scaled[:, cols], op=ADD
                 )
                 nc.sync.dma_start(out=out[b][:, cols], in_=result[:, cols])
+
+        def front_step(b):
+            return max(b - LEAD, b // PAIR)
 
         run_of_first = {}
         for r in range(2, len(RUNS)):
@@ -234,26 +246,40 @@ def tile_gatblock_pa_kernel(
         mix(0, None)
         quantise_agg(0)
         mix(1, None)
-        copy_run(1, transpose_run(1))
-        pending_run = 1
 
         for s in range(SAMPLES):
-            products(s)
-            woven = None
+            fronts = []
             for b in range(PAIR, SAMPLES):
-                if max(b - LEAD, b // PAIR - 1) == s:
-                    mix(b, run_of_first.get(b))
-                    if b in run_of_first:
-                        woven = run_of_first[b]
+                if front_step(b) == s:
+                    fronts.append(b)
+            due = []
+            o_ps = product_o(s)
+            if s == 0:
+                m_ps = psum.tile([P, D_OUT], F32, tag="agg")
+                nc.tensor.matmul(out=m_ps[:], lhsT=ones[:], rhs=vec_rows[:, 0, :], start=True, stop=True)
+                nc.scalar.copy(out=m_all[:], in_=m_ps[:])
+            elif fronts:
+                mix(fronts[0], run_of_first.get(fronts[0]))
+            g_ps = product_g(s)
+            if s == 0:
+                copy_run(1, transpose_run(1))
+                due.append(1)
+            for b in fronts[1:]:
+                mix(b, run_of_first.get(b))
+            for b in fronts:
+                if b in run_of_first:
+                    due.append(run_of_first[b])
             last = s == SAMPLES - 1
-            empty_banks(s, 2 if last else 1)
-            for b in range(1, SAMPLES):
-                if max(b - 2, 0) == s:
+            biased = add_bias(o_ps)
+            if s == 0:
+                quantise_agg(1)
+            scaled = scale_g(g_ps, 2 if last else 1)
+            for b in range(PAIR, SAMPLES):
+                if max(b - 2, front_step(b)) == s:
                     quantise_agg(b)
-            if pending_run is not None:
-                quantise_run(pending_run)
-            pending_run = woven
+            for r in due:
+                quantise_run(r)
             if last:
-                finish(s, nc.vector, 2)
+                finish(s, biased, scaled, nc.vector, 2)
             else:
-                finish(s, nc.gpsimd, 1)
+                finish(s, biased, scaled, nc.gpsimd, 1)

@@ -21,6 +21,7 @@ D_OUT = 512
 PAIR = 2
 LEAD = 3
 RUNS = ((0, 2), (2, 2), (4, 2), (6, 2), (8, 4))
+WARM_UP = 12
 
 FLOPS = 2 * 2 * SAMPLES * P * D * D_OUT + 2 * SAMPLES * P * P * D
 
@@ -110,6 +111,10 @@ def tile_gatblock_pa_kernel(
         load_o(4)
         load_h(4)
         load_h(5)
+
+        warm_ps = psum.tile([P, P], F32, tag="o")
+        for i in range(WARM_UP):
+            nc.tensor.matmul(out=warm_ps[:], lhsT=ident_bf16[:], rhs=ident_bf16[:], start=True, stop=True)
 
         aT_ps = psum.tile([P, P], BF16, tag="xt")
         nc.tensor.transpose(aT_ps[:], a_sb[:], ident_bf16[:])

@@ -22,6 +22,7 @@ PAIR = 2
 LEAD = 3
 RUNS = ((0, 2), (2, 2), (4, 2), (6, 2), (8, 4))
 WARM_UP = 12
+FILL = 3
 
 FLOPS = 2 * 2 * SAMPLES * P * D * D_OUT + 2 * SAMPLES * P * P * D
 
@@ -263,13 +264,14 @@ def tile_gatblock_pa_kernel(
                 m_ps = psum.tile([P, D_OUT], F32, tag="agg")
                 nc.tensor.matmul(out=m_ps[:], lhsT=ones[:], rhs=vec_rows[:, 0, :], start=True, stop=True)
                 nc.scalar.copy(out=m_all[:], in_=m_ps[:])
-            elif fronts:
-                mix(fronts[0], run_of_first.get(fronts[0]))
+            early = fronts[:1] if s < FILL else []
+            for b in early:
+                mix(b, run_of_first.get(b))
             g_ps = product_g(s)
             if s == 0:
                 copy_run(1, transpose_run(1))
                 due.append(1)
-            for b in fronts[1:]:
+            for b in fronts[len(early) :]:
                 mix(b, run_of_first.get(b))
             for b in fronts:
                 if b in run_of_first:

@@ -264,15 +264,18 @@ def tile_gatblock_pa_kernel(
                 m_ps = psum.tile([P, D_OUT], F32, tag="agg")
                 nc.tensor.matmul(out=m_ps[:], lhsT=ones[:], rhs=vec_rows[:, 0, :], start=True, stop=True)
                 nc.scalar.copy(out=m_all[:], in_=m_ps[:])
+            for b in fronts:
+                if b in run_of_first:
+                    copy_run(run_of_first[b], transpose_run(run_of_first[b]))
             early = fronts[:1] if s < FILL else []
             for b in early:
-                mix(b, run_of_first.get(b))
+                mix(b, None)
             g_ps = product_g(s)
             if s == 0:
                 copy_run(1, transpose_run(1))
                 due.append(1)
             for b in fronts[len(early) :]:
-                mix(b, run_of_first.get(b))
+                mix(b, None)
             for b in fronts:
                 if b in run_of_first:
                     due.append(run_of_first[b])

@@ -259,14 +259,14 @@ def tile_gatblock_pa_kernel(
                 if front_step(b) == s:
                     fronts.append(b)
             due = []
+            for b in fronts:
+                if b in run_of_first:
+                    copy_run(run_of_first[b], transpose_run(run_of_first[b]))
             o_ps = product_o(s)
             if s == 0:
                 m_ps = psum.tile([P, D_OUT], F32, tag="agg")
                 nc.tensor.matmul(out=m_ps[:], lhsT=ones[:], rhs=vec_rows[:, 0, :], start=True, stop=True)
                 nc.scalar.copy(out=m_all[:], in_=m_ps[:])
-            for b in fronts:
-                if b in run_of_first:
-                    copy_run(run_of_first[b], transpose_run(run_of_first[b]))
             early = fronts[:1] if s < FILL else []
             for b in early:
                 mix(b, None)

@@ -19,7 +19,7 @@ SAMPLES = 12
 D = 512
 D_OUT = 512
 PAIR = 2
-LEAD = 3
+LEAD = 2
 RUNS = ((0, 2), (2, 2), (4, 2), (6, 2), (8, 4))
 WARM_UP = 12
 FILL = 3

@@ -20,7 +20,8 @@ D = 512
 D_OUT = 512
 PAIR = 2
 LEAD = 2
-RUNS = ((0, 2), (2, 2), (4, 2), (6, 2), (8, 4))
+RUNS = ((0, 1), (1, 1), (2, 2), (4, 2), (6, 2), (8, 4))
+O_LOADS = ((0, 2), (2, 2), (4, 2), (6, 2), (8, 4))
 WARM_UP = 12
 FILL = 3
 
@@ -56,7 +57,7 @@ def tile_gatblock_pa_kernel(
         pools.enter_context(tc.manual_schedule())
 
         vec_rows = const.tile([P, 2, D_OUT], BF16)
-        nc.vector.memset(vec_rows[:], 0.0)
+        nc.vector.memset(vec_rows[:].bitcast(I32), 0)
         w_planes = const.tile([P, 2, D_OUT], U8, align_bytes=64)
         nc.vector.memset(w_planes[:].bitcast(I32), 0)
         ones = const.tile([P, P], BF16)
@@ -77,7 +78,7 @@ def tile_gatblock_pa_kernel(
             h_sb = const.tile([P, PAIR, D], BF16, name="h_sb%d" % c)
             h_tiles.append(h_sb)
         o_tiles = []
-        for first, count in RUNS:
+        for first, count in O_LOADS:
             o_sb = const.tile([P, count, D], BF16, name="o_sb%d" % first)
             o_tiles.append(o_sb)
 
@@ -86,23 +87,23 @@ def tile_gatblock_pa_kernel(
             nc.sync.dma_start(out=h_tiles[c][:], in_=h_norm[rows].rearrange("b n d -> n b d"))
 
         def load_o(r):
-            first, count = RUNS[r]
+            first, count = O_LOADS[r]
             nc.sync.dma_start(
                 out=o_tiles[r][:], in_=o_attn[first : first + count].rearrange("b n d -> n b d")
             )
 
         nc.sync.dma_start(out=a_sb[:], in_=a_gcn)
-        load_o(0)
-        load_h(0)
-        nc.sync.dma_start(out=vec_rows[0:1, 1, :], in_=b_proj.unsqueeze(0))
-        load_words(nc, w_proj_words, proj_words[:])
-        for r in range(3):
-            load_scales(nc, w_proj_scales, w_planes[:, 1, :], r)
-        load_scales(nc, w_proj_scales, w_planes[:, 1, :], 3)
         nc.sync.dma_start(out=vec_rows[0:1, 0, :], in_=gcn_m.unsqueeze(0))
-        load_words(nc, gcn_w_words, gcn_words[:])
-        for r in range(4):
+        nc.sync.dma_start(out=vec_rows[0:1, 1, :], in_=b_proj.unsqueeze(0))
+        for r in range(3):
             load_scales(nc, gcn_w_scales, w_planes[:, 0, :], r)
+        load_h(0)
+        load_o(0)
+        load_scales(nc, gcn_w_scales, w_planes[:, 0, :], 3)
+        load_words(nc, gcn_w_words, gcn_words[:])
+        load_words(nc, w_proj_words, proj_words[:])
+        for r in range(4):
+            load_scales(nc, w_proj_scales, w_planes[:, 1, :], r)
         load_o(1)
         load_h(1)
         load_o(2)
@@ -121,11 +122,14 @@ def tile_gatblock_pa_kernel(
         nc.tensor.transpose(aT_ps[:], a_sb[:], ident_bf16[:])
         aT_sb = const.tile([P, P], BF16)
         nc.vector.tensor_copy(out=aT_sb[:], in_=aT_ps[:])
+        m_ps = psum.tile([P, D_OUT], F32, tag="agg")
+        nc.tensor.matmul(out=m_ps[:], lhsT=ones[:], rhs=vec_rows[:, 0, :], start=True, stop=True)
+        m_all = const.tile([P, D_OUT], F32)
+        nc.scalar.copy(out=m_all[:], in_=m_ps[:])
         b_ps = psum.tile([P, D_OUT], F32, tag="g")
         nc.tensor.matmul(out=b_ps[:], lhsT=ones[:], rhs=vec_rows[:, 1, :], start=True, stop=True)
         b_all = const.tile([P, D_OUT], F32)
         nc.vector.tensor_copy(out=b_all[:], in_=b_ps[:])
-        m_all = const.tile([P, D_OUT], F32)
 
         agg_codes = const.tile([P, SAMPLES, P], U32, align_bytes=64)
         agg_scales = const.tile([P, SAMPLES, P], U8, align_bytes=64)
@@ -133,29 +137,34 @@ def tile_gatblock_pa_kernel(
         o_scales = const.tile([P, SAMPLES, P], U8, align_bytes=64)
         agg_grouped = {}
         o_grouped = {}
+        o_source = {}
+        for r in range(len(O_LOADS)):
+            for j in range(O_LOADS[r][1]):
+                o_source[O_LOADS[r][0] + j] = o_tiles[r][:, j, :]
 
         def transpose_run(r):
             first, count = RUNS[r]
-            grouped = stage.tile([P, count, P, PACK], BF16, tag="o_grouped", bufs=2, align_bytes=64)
+            grouped = stage.tile([P, count, P, PACK], BF16, tag="o_grouped", bufs=3, align_bytes=64)
             o_grouped[r] = grouped
             xts = []
-            for q in range(count // PAIR):
+            for q in range(0, count, PAIR):
                 xt_ps = psum.tile([P, PAIR, 2, P], F32, tag="xt")
                 xts.append(xt_ps)
-                for j in range(PAIR):
-                    words = o_tiles[r][:, q * PAIR + j, :].bitcast(F32)
+                for j in range(min(PAIR, count - q)):
+                    words = o_source[first + q + j].bitcast(F32)
                     for u in range(2):
                         nc.tensor.transpose(
                             xt_ps[:, j, u, :], words[:, u : D // 2 : 2], ident_f32[:]
                         )
             return xts
 
-        def copy_run(r, xts):
+        def copy_run(r, xts, copy):
+            count = RUNS[r][1]
             for q in range(len(xts)):
-                copy = nc.vector.tensor_copy if r == 0 else nc.scalar.copy
+                n = min(PAIR, count - q * PAIR)
                 copy(
-                    out=o_grouped[r][:, q * PAIR : (q + 1) * PAIR, :, :].bitcast(F32),
-                    in_=xts[q][:].rearrange("p j u i -> p j i u"),
+                    out=o_grouped[r][:, q * PAIR : q * PAIR + n, :, :].bitcast(F32),
+                    in_=xts[q][:, 0:n, :, :].rearrange("p j u i -> p j i u"),
                 )
 
         def quantise_run(r):
@@ -166,22 +175,16 @@ def tile_gatblock_pa_kernel(
                 in_=o_grouped[r][:].rearrange("p b i t -> p (b i t)"),
             )
 
-        def mix(b, run):
+        def mix(b):
             h = h_tiles[b // PAIR][:, b % PAIR, :]
             agg_ps = psum.tile([P, PACK, P], F32, tag="agg")
-            xts = []
             for t in range(PACK):
-                if t == PACK // 2 and run is not None:
-                    xts = transpose_run(run)
                 nc.tensor.matmul(
                     out=agg_ps[:, t, :], lhsT=h[:, t:D:PACK], rhs=aT_sb[:], start=True, stop=True
                 )
-            if run is not None:
-                copy_run(run, xts)
             grouped = stage.tile([P, P, PACK], BF16, tag="agg_grouped", align_bytes=64)
             agg_grouped[b] = grouped
             nc.scalar.copy(out=grouped[:], in_=agg_ps[:].rearrange("p t i -> p i t"))
-
         def quantise_agg(b):
             nc.vector.quantize_mx(
                 out=agg_codes[:, b, :].bitcast(FP8X4),
@@ -244,14 +247,14 @@ def tile_gatblock_pa_kernel(
             return max(b - LEAD, b // PAIR)
 
         run_of_first = {}
-        for r in range(2, len(RUNS)):
+        for r in range(3, len(RUNS)):
             run_of_first[RUNS[r][0]] = r
 
-        copy_run(0, transpose_run(0))
-        quantise_run(0)
-        mix(0, None)
+        mix(0)
+        copy_run(0, transpose_run(0), nc.vector.tensor_copy)
         quantise_agg(0)
-        mix(1, None)
+        quantise_run(0)
+        mix(1)
 
         for s in range(SAMPLES):
             fronts = []
@@ -261,29 +264,39 @@ def tile_gatblock_pa_kernel(
             due = []
             for b in fronts:
                 if b in run_of_first:
-                    copy_run(run_of_first[b], transpose_run(run_of_first[b]))
-            o_ps = product_o(s)
-            if s == 0:
-                m_ps = psum.tile([P, D_OUT], F32, tag="agg")
-                nc.tensor.matmul(out=m_ps[:], lhsT=ones[:], rhs=vec_rows[:, 0, :], start=True, stop=True)
-                nc.scalar.copy(out=m_all[:], in_=m_ps[:])
+                    copy_run(run_of_first[b], transpose_run(run_of_first[b]), nc.scalar.copy)
+            g_first = s < 2
+            if g_first:
+                g_ps = product_g(s)
+            else:
+                o_ps = product_o(s)
             early = fronts[:1] if s < FILL else []
             for b in early:
-                mix(b, None)
-            g_ps = product_g(s)
+                mix(b)
+            if g_first:
+                o_ps = product_o(s)
+            else:
+                g_ps = product_g(s)
             if s == 0:
-                copy_run(1, transpose_run(1))
-                due.append(1)
+                copy_run(1, transpose_run(1), nc.scalar.copy)
+                copy_run(2, transpose_run(2), nc.scalar.copy)
             for b in fronts[len(early) :]:
-                mix(b, None)
+                mix(b)
             for b in fronts:
                 if b in run_of_first:
                     due.append(run_of_first[b])
             last = s == SAMPLES - 1
-            biased = add_bias(o_ps)
-            if s == 0:
-                quantise_agg(1)
-            scaled = scale_g(g_ps, 2 if last else 1)
+            if g_first:
+                scaled = scale_g(g_ps, 1)
+                if s == 0:
+                    quantise_agg(1)
+                biased = add_bias(o_ps)
+                if s == 0:
+                    quantise_run(1)
+                    due.append(2)
+            else:
+                biased = add_bias(o_ps)
+                scaled = scale_g(g_ps, 2 if last else 1)
             for b in range(PAIR, SAMPLES):
                 if max(b - 2, front_step(b)) == s:
                     quantise_agg(b)

@@ -21,8 +21,9 @@ D_OUT = 512
 PAIR = 2
 LEAD = 2
 RUNS = ((0, 1), (1, 1), (2, 2), (4, 2), (6, 2), (8, 4))
-O_LOADS = ((0, 2), (2, 2), (4, 2), (6, 2), (8, 4))
-WARM_UP = 12
+O_LOADS = ((0, 4), (4, 2), (6, 2), (8, 4))
+H_LOADS = ((0, 2), (2, 2), (4, 2), (6, 2), (8, 2), (10, 2))
+WARM_UP = 7
 FILL = 3
 
 FLOPS = 2 * 2 * SAMPLES * P * D * D_OUT + 2 * SAMPLES * P * P * D
@@ -58,8 +59,10 @@ def tile_gatblock_pa_kernel(
 
         vec_rows = const.tile([P, 2, D_OUT], BF16)
         nc.vector.memset(vec_rows[:].bitcast(I32), 0)
-        w_planes = const.tile([P, 2, D_OUT], U8, align_bytes=64)
-        nc.vector.memset(w_planes[:].bitcast(I32), 0)
+        gcn_plane = const.tile([P, D_OUT], U8, align_bytes=64)
+        nc.vector.memset(gcn_plane[:].bitcast(I32), 0)
+        proj_plane = const.tile([P, D_OUT], U8, align_bytes=64)
+        nc.vector.memset(proj_plane[:].bitcast(I32), 0)
         ones = const.tile([P, P], BF16)
         nc.vector.memset(ones[:], 1.0)
         warm = const.tile([P, 2], F32)
@@ -74,17 +77,19 @@ def tile_gatblock_pa_kernel(
         gcn_words = const.tile([P, 2 * D_OUT], U8, align_bytes=64)
         proj_words = const.tile([P, 2 * D_OUT], U8, align_bytes=64)
         h_tiles = []
-        for c in range(SAMPLES // PAIR):
-            h_sb = const.tile([P, PAIR, D], BF16, name="h_sb%d" % c)
+        for first, count in H_LOADS:
+            h_sb = const.tile([P, count, D], BF16, name="h_sb%d" % first)
             h_tiles.append(h_sb)
         o_tiles = []
         for first, count in O_LOADS:
             o_sb = const.tile([P, count, D], BF16, name="o_sb%d" % first)
             o_tiles.append(o_sb)
 
-        def load_h(c):
-            rows = slice(c * PAIR, (c + 1) * PAIR)
-            nc.sync.dma_start(out=h_tiles[c][:], in_=h_norm[rows].rearrange("b n d -> n b d"))
+        def load_h(r):
+            first, count = H_LOADS[r]
+            nc.sync.dma_start(
+                out=h_tiles[r][:], in_=h_norm[first : first + count].rearrange("b n d -> n b d")
+            )
 
         def load_o(r):
             first, count = O_LOADS[r]
@@ -93,43 +98,45 @@ def tile_gatblock_pa_kernel(
             )
 
         nc.sync.dma_start(out=a_sb[:], in_=a_gcn)
-        nc.sync.dma_start(out=vec_rows[0:1, 0, :], in_=gcn_m.unsqueeze(0))
-        nc.sync.dma_start(out=vec_rows[0:1, 1, :], in_=b_proj.unsqueeze(0))
-        for r in range(3):
-            load_scales(nc, gcn_w_scales, w_planes[:, 0, :], r)
         load_h(0)
-        load_o(0)
-        load_scales(nc, gcn_w_scales, w_planes[:, 0, :], 3)
         load_words(nc, gcn_w_words, gcn_words[:])
+        nc.sync.dma_start(out=vec_rows[0:1, 0, :], in_=gcn_m.unsqueeze(0))
+        load_scales(nc, gcn_w_scales, gcn_plane[:], 0)
+        load_scales(nc, gcn_w_scales, gcn_plane[:], 1)
+        load_scales(nc, gcn_w_scales, gcn_plane[:], 2)
+        load_scales(nc, gcn_w_scales, gcn_plane[:], 3)
+        load_o(0)
+        nc.sync.dma_start(out=vec_rows[0:1, 1, :], in_=b_proj.unsqueeze(0))
         load_words(nc, w_proj_words, proj_words[:])
-        for r in range(4):
-            load_scales(nc, w_proj_scales, w_planes[:, 1, :], r)
-        load_o(1)
+        load_scales(nc, w_proj_scales, proj_plane[:], 0)
+        load_scales(nc, w_proj_scales, proj_plane[:], 1)
+        load_scales(nc, w_proj_scales, proj_plane[:], 2)
+        load_scales(nc, w_proj_scales, proj_plane[:], 3)
         load_h(1)
-        load_o(2)
+        load_o(1)
         load_h(2)
-        load_o(3)
+        load_o(2)
         load_h(3)
-        load_o(4)
+        load_o(3)
         load_h(4)
         load_h(5)
-
         warm_ps = psum.tile([P, P], F32, tag="o")
         for i in range(WARM_UP):
             nc.tensor.matmul(out=warm_ps[:], lhsT=ident_bf16[:], rhs=ident_bf16[:], start=True, stop=True)
 
-        aT_ps = psum.tile([P, P], BF16, tag="xt")
-        nc.tensor.transpose(aT_ps[:], a_sb[:], ident_bf16[:])
         aT_sb = const.tile([P, P], BF16)
-        nc.vector.tensor_copy(out=aT_sb[:], in_=aT_ps[:])
-        m_ps = psum.tile([P, D_OUT], F32, tag="agg")
-        nc.tensor.matmul(out=m_ps[:], lhsT=ones[:], rhs=vec_rows[:, 0, :], start=True, stop=True)
         m_all = const.tile([P, D_OUT], F32)
-        nc.scalar.copy(out=m_all[:], in_=m_ps[:])
-        b_ps = psum.tile([P, D_OUT], F32, tag="g")
-        nc.tensor.matmul(out=b_ps[:], lhsT=ones[:], rhs=vec_rows[:, 1, :], start=True, stop=True)
         b_all = const.tile([P, D_OUT], F32)
-        nc.vector.tensor_copy(out=b_all[:], in_=b_ps[:])
+
+        def transpose_a():
+            aT_ps = psum.tile([P, P], BF16, tag="xt")
+            nc.tensor.transpose(aT_ps[:], a_sb[:], ident_bf16[:])
+            nc.vector.tensor_copy(out=aT_sb[:], in_=aT_ps[:])
+
+        def spread(row, tag, dest, copy):
+            row_ps = psum.tile([P, D_OUT], F32, tag=tag)
+            nc.tensor.matmul(out=row_ps[:], lhsT=ones[:], rhs=vec_rows[:, row, :], start=True, stop=True)
+            copy(out=dest[:], in_=row_ps[:])
 
         agg_codes = const.tile([P, SAMPLES, P], U32, align_bytes=64)
         agg_scales = const.tile([P, SAMPLES, P], U8, align_bytes=64)
@@ -141,6 +148,11 @@ def tile_gatblock_pa_kernel(
         for r in range(len(O_LOADS)):
             for j in range(O_LOADS[r][1]):
                 o_source[O_LOADS[r][0] + j] = o_tiles[r][:, j, :]
+
+        h_source = {}
+        for r in range(len(H_LOADS)):
+            for j in range(H_LOADS[r][1]):
+                h_source[H_LOADS[r][0] + j] = h_tiles[r][:, j, :]
 
         def transpose_run(r):
             first, count = RUNS[r]
@@ -176,7 +188,7 @@ def tile_gatblock_pa_kernel(
             )
 
         def mix(b):
-            h = h_tiles[b // PAIR][:, b % PAIR, :]
+            h = h_source[b]
             agg_ps = psum.tile([P, PACK, P], F32, tag="agg")
             for t in range(PACK):
                 nc.tensor.matmul(
@@ -199,7 +211,7 @@ def tile_gatblock_pa_kernel(
                 lhsT=o_codes[:, b, :].bitcast(FP8X4),
                 lhsT_scale=o_scales[:, b, :],
                 rhs=proj_words[:].bitcast(FP4X4),
-                rhs_scale=w_planes[:, 1, :],
+                rhs_scale=proj_plane[:],
                 start=True,
                 stop=True,
             )
@@ -212,7 +224,7 @@ def tile_gatblock_pa_kernel(
                 lhsT=agg_codes[:, b, :].bitcast(FP8X4),
                 lhsT_scale=agg_scales[:, b, :],
                 rhs=gcn_words[:].bitcast(FP4X4),
-                rhs_scale=w_planes[:, 0, :],
+                rhs_scale=gcn_plane[:],
                 start=True,
                 stop=True,
             )
@@ -250,54 +262,57 @@ def tile_gatblock_pa_kernel(
         for r in range(3, len(RUNS)):
             run_of_first[RUNS[r][0]] = r
 
+        transpose_a()
         mix(0)
-        copy_run(0, transpose_run(0), nc.vector.tensor_copy)
-        quantise_agg(0)
-        quantise_run(0)
         mix(1)
+        quantise_agg(0)
+        spread(0, "g", m_all, nc.vector.tensor_copy)
+        g_ps0 = product_g(0)
+        quantise_agg(1)
+        scaled0 = scale_g(g_ps0, 1)
+        g_ps1 = product_g(1)
+        scaled1 = scale_g(g_ps1, 1)
+        copy_run(0, transpose_run(0), nc.scalar.copy)
+        quantise_run(0)
+        copy_run(1, transpose_run(1), nc.vector.tensor_copy)
+        quantise_run(1)
+        spread(1, "o", b_all, nc.scalar.copy)
+        copy_run(2, transpose_run(2), nc.scalar.copy)
+        o_ps0 = product_o(0)
+        mix(2)
+        o_ps1 = product_o(1)
+        mix(3)
+        biased0 = add_bias(o_ps0)
+        quantise_run(2)
+        finish(0, biased0, scaled0, nc.gpsimd, 1)
+        biased1 = add_bias(o_ps1)
+        quantise_agg(2)
+        quantise_agg(3)
+        finish(1, biased1, scaled1, nc.gpsimd, 1)
 
-        for s in range(SAMPLES):
+        for s in range(2, SAMPLES):
             fronts = []
-            for b in range(PAIR, SAMPLES):
+            for b in range(4, SAMPLES):
                 if front_step(b) == s:
                     fronts.append(b)
             due = []
             for b in fronts:
                 if b in run_of_first:
                     copy_run(run_of_first[b], transpose_run(run_of_first[b]), nc.scalar.copy)
-            g_first = s < 2
-            if g_first:
-                g_ps = product_g(s)
-            else:
-                o_ps = product_o(s)
+            o_ps = product_o(s)
             early = fronts[:1] if s < FILL else []
             for b in early:
                 mix(b)
-            if g_first:
-                o_ps = product_o(s)
-            else:
-                g_ps = product_g(s)
-            if s == 0:
-                copy_run(1, transpose_run(1), nc.scalar.copy)
-                copy_run(2, transpose_run(2), nc.scalar.copy)
+            g_ps = product_g(s)
             for b in fronts[len(early) :]:
                 mix(b)
             for b in fronts:
                 if b in run_of_first:
                     due.append(run_of_first[b])
             last = s == SAMPLES - 1
-            if g_first:
-                scaled = scale_g(g_ps, 1)
-                if s == 0:
-                    quantise_agg(1)
-                biased = add_bias(o_ps)
-                if s == 0:
-                    quantise_run(1)
-                    due.append(2)
-            else:
-                biased = add_bias(o_ps)
-                scaled = scale_g(g_ps, 2 if last else 1)
-            for b in range(PAIR, SAMPLES):
+            biased = add_bias(o_ps)
+            scaled = scale_g(g_ps, 2 if last else 1)
+            for b in range(4, SAMPLES):
                 if max(b - 2, front_step(b)) == s:
                     quantise_agg(b)
             for r in due:

from contextlib import ExitStack

import concourse.mybir as mybir
from concourse.masks import make_identity

F32 = mybir.dt.float32
BF16 = mybir.dt.bfloat16
I32 = mybir.dt.int32
U32 = mybir.dt.uint32
U8 = mybir.dt.uint8
FP8X4 = mybir.dt.float8_e4m3fn_x4
FP4X4 = mybir.dt.float4_e2m1fn_x4
MULT = mybir.AluOpType.mult
ADD = mybir.AluOpType.add

P = 128
PACK = 4
SAMPLES = 12
D = 512
D_OUT = 512
PAIR = 2
LEAD = 2
RUNS = ((0, 1), (1, 1), (2, 2), (4, 2), (6, 2), (8, 4))
O_LOADS = ((0, 4), (4, 2), (6, 2), (8, 4))
H_LOADS = ((0, 2), (2, 2), (4, 2), (6, 2), (8, 2), (10, 2))
WARM_UP = 7
FILL = 3

FLOPS = 2 * 2 * SAMPLES * P * D * D_OUT + 2 * SAMPLES * P * P * D


def load_words(nc, words_dram, words):
    nc.sync.dma_start(out=words.bitcast(I32), in_=words_dram[0].bitcast(I32))


def load_scales(nc, scales_dram, plane, r):
    nc.sync.dma_start(out=plane[r:P:32, :].bitcast(I32), in_=scales_dram[0, r:16:4, :].bitcast(I32))


def tile_gatblock_pa_kernel(
    tc,
    h_norm,
    o_attn,
    a_gcn,
    w_proj_words,
    w_proj_scales,
    b_proj,
    gcn_w_words,
    gcn_w_scales,
    gcn_m,
    out,
):
    nc = tc.nc
    with ExitStack() as pools:
        const = pools.enter_context(tc.tile_pool(name="const", bufs=1))
        stage = pools.enter_context(tc.tile_pool(name="stage", bufs=4))
        psum = pools.enter_context(tc.psum_pool(name="psum", bufs=2))
        pools.enter_context(tc.manual_schedule())

        vec_rows = const.tile([P, 2, D_OUT], BF16)
        nc.vector.memset(vec_rows[:].bitcast(I32), 0)
        gcn_plane = const.tile([P, D_OUT], U8, align_bytes=64)
        nc.vector.memset(gcn_plane[:].bitcast(I32), 0)
        proj_plane = const.tile([P, D_OUT], U8, align_bytes=64)
        nc.vector.memset(proj_plane[:].bitcast(I32), 0)
        ones = const.tile([P, P], BF16)
        nc.vector.memset(ones[:], 1.0)
        warm = const.tile([P, 2], F32)
        nc.gpsimd.memset(warm[:, 0:1], 0.0)
        nc.scalar.copy(out=warm[:, 1:2], in_=warm[:, 0:1])
        ident_bf16 = const.tile([P, P], BF16)
        make_identity(nc, ident_bf16[:])
        ident_f32 = const.tile([P, P], F32)
        make_identity(nc, ident_f32[:])

        a_sb = const.tile([P, P], BF16)
        gcn_words = const.tile([P, 2 * D_OUT], U8, align_bytes=64)
        proj_words = const.tile([P, 2 * D_OUT], U8, align_bytes=64)
        h_tiles = []
        for first, count in H_LOADS:
            h_sb = const.tile([P, count, D], BF16, name="h_sb%d" % first)
            h_tiles.append(h_sb)
        o_tiles = []
        for first, count in O_LOADS:
            o_sb = const.tile([P, count, D], BF16, name="o_sb%d" % first)
            o_tiles.append(o_sb)

        def load_h(r):
            first, count = H_LOADS[r]
            nc.sync.dma_start(
                out=h_tiles[r][:], in_=h_norm[first : first + count].rearrange("b n d -> n b d")
            )

        def load_o(r):
            first, count = O_LOADS[r]
            nc.sync.dma_start(
                out=o_tiles[r][:], in_=o_attn[first : first + count].rearrange("b n d -> n b d")
            )

        nc.sync.dma_start(out=a_sb[:], in_=a_gcn)
        load_h(0)
        load_words(nc, gcn_w_words, gcn_words[:])
        nc.sync.dma_start(out=vec_rows[0:1, 0, :], in_=gcn_m.unsqueeze(0))
        load_scales(nc, gcn_w_scales, gcn_plane[:], 0)
        load_scales(nc, gcn_w_scales, gcn_plane[:], 1)
        load_scales(nc, gcn_w_scales, gcn_plane[:], 2)
        load_scales(nc, gcn_w_scales, gcn_plane[:], 3)
        load_o(0)
        nc.sync.dma_start(out=vec_rows[0:1, 1, :], in_=b_proj.unsqueeze(0))
        load_words(nc, w_proj_words, proj_words[:])
        load_scales(nc, w_proj_scales, proj_plane[:], 0)
        load_scales(nc, w_proj_scales, proj_plane[:], 1)
        load_scales(nc, w_proj_scales, proj_plane[:], 2)
        load_scales(nc, w_proj_scales, proj_plane[:], 3)
        load_h(1)
        load_o(1)
        load_h(2)
        load_o(2)
        load_h(3)
        load_o(3)
        load_h(4)
        load_h(5)
        warm_ps = psum.tile([P, P], F32, tag="o")
        for i in range(WARM_UP):
            nc.tensor.matmul(out=warm_ps[:], lhsT=ident_bf16[:], rhs=ident_bf16[:], start=True, stop=True)

        aT_sb = const.tile([P, P], BF16)
        m_all = const.tile([P, D_OUT], F32)
        b_all = const.tile([P, D_OUT], F32)

        def transpose_a():
            aT_ps = psum.tile([P, P], BF16, tag="xt")
            nc.tensor.transpose(aT_ps[:], a_sb[:], ident_bf16[:])
            nc.vector.tensor_copy(out=aT_sb[:], in_=aT_ps[:])

        def spread(row, tag, dest, copy):
            row_ps = psum.tile([P, D_OUT], F32, tag=tag)
            nc.tensor.matmul(out=row_ps[:], lhsT=ones[:], rhs=vec_rows[:, row, :], start=True, stop=True)
            copy(out=dest[:], in_=row_ps[:])

        agg_codes = const.tile([P, SAMPLES, P], U32, align_bytes=64)
        agg_scales = const.tile([P, SAMPLES, P], U8, align_bytes=64)
        o_codes = const.tile([P, SAMPLES, P], U32, align_bytes=64)
        o_scales = const.tile([P, SAMPLES, P], U8, align_bytes=64)
        agg_grouped = {}
        o_grouped = {}
        o_source = {}
        for r in range(len(O_LOADS)):
            for j in range(O_LOADS[r][1]):
                o_source[O_LOADS[r][0] + j] = o_tiles[r][:, j, :]

        h_source = {}
        for r in range(len(H_LOADS)):
            for j in range(H_LOADS[r][1]):
                h_source[H_LOADS[r][0] + j] = h_tiles[r][:, j, :]

        def transpose_run(r):
            first, count = RUNS[r]
            grouped = stage.tile([P, count, P, PACK], BF16, tag="o_grouped", bufs=3, align_bytes=64)
            o_grouped[r] = grouped
            xts = []
            for q in range(0, count, PAIR):
                xt_ps = psum.tile([P, PAIR, 2, P], F32, tag="xt")
                xts.append(xt_ps)
                for j in range(min(PAIR, count - q)):
                    words = o_source[first + q + j].bitcast(F32)
                    for u in range(2):
                        nc.tensor.transpose(
                            xt_ps[:, j, u, :], words[:, u : D // 2 : 2], ident_f32[:]
                        )
            return xts

        def copy_run(r, xts, copy):
            count = RUNS[r][1]
            for q in range(len(xts)):
                n = min(PAIR, count - q * PAIR)
                copy(
                    out=o_grouped[r][:, q * PAIR : q * PAIR + n, :, :].bitcast(F32),
                    in_=xts[q][:, 0:n, :, :].rearrange("p j u i -> p j i u"),
                )

        def quantise_run(r):
            first, count = RUNS[r]
            nc.vector.quantize_mx(
                out=o_codes[:, first : first + count, :].rearrange("p b i -> p (b i)").bitcast(FP8X4),
                scales=o_scales[:, first : first + count, :].rearrange("p b i -> p (b i)"),
                in_=o_grouped[r][:].rearrange("p b i t -> p (b i t)"),
            )

        def mix(b):
            h = h_source[b]
            agg_ps = psum.tile([P, PACK, P], F32, tag="agg")
            for t in range(PACK):
                nc.tensor.matmul(
                    out=agg_ps[:, t, :], lhsT=h[:, t:D:PACK], rhs=aT_sb[:], start=True, stop=True
                )
            grouped = stage.tile([P, P, PACK], BF16, tag="agg_grouped", align_bytes=64)
            agg_grouped[b] = grouped
            nc.scalar.copy(out=grouped[:], in_=agg_ps[:].rearrange("p t i -> p i t"))
        def quantise_agg(b):
            nc.vector.quantize_mx(
                out=agg_codes[:, b, :].bitcast(FP8X4),
                scales=agg_scales[:, b, :],
                in_=agg_grouped[b][:].rearrange("p i t -> p (i t)"),
            )

        def product_o(b):
            o_ps = psum.tile([P, D_OUT], F32, tag="o")
            nc.tensor.matmul_mx(
                out=o_ps[:],
                lhsT=o_codes[:, b, :].bitcast(FP8X4),
                lhsT_scale=o_scales[:, b, :],
                rhs=proj_words[:].bitcast(FP4X4),
                rhs_scale=proj_plane[:],
                start=True,
                stop=True,
            )
            return o_ps

        def product_g(b):
            g_ps = psum.tile([P, D_OUT], F32, tag="g")
            nc.tensor.matmul_mx(
                out=g_ps[:],
                lhsT=agg_codes[:, b, :].bitcast(FP8X4),
                lhsT_scale=agg_scales[:, b, :],
                rhs=gcn_words[:].bitcast(FP4X4),
                rhs_scale=gcn_plane[:],
                start=True,
                stop=True,
            )
            return g_ps

        def add_bias(o_ps):
            biased = stage.tile([P, D_OUT], F32, tag="biased")
            nc.vector.tensor_tensor(out=biased[:], in0=o_ps[:], in1=b_all[:], op=ADD)
            return biased

        def scale_g(g_ps, pieces):
            scaled = stage.tile([P, D_OUT], F32, tag="scaled")
            width = D_OUT // pieces
            for c in range(pieces):
                cols = slice(c * width, (c + 1) * width)
                nc.vector.tensor_tensor(
                    out=scaled[:, cols], in0=g_ps[:, cols], in1=m_all[:, cols], op=MULT
                )
            return scaled

        def finish(b, biased, scaled, engine, pieces):
            result = stage.tile([P, D_OUT], F32, tag="result")
            width = D_OUT // pieces
            for c in range(pieces):
                cols = slice(c * width, (c + 1) * width)
                engine.tensor_tensor(
                    out=result[:, cols], in0=biased[:, cols], in1=scaled[:, cols], op=ADD
                )
                nc.sync.dma_start(out=out[b][:, cols], in_=result[:, cols])

        def front_step(b):
            return max(b - LEAD, b // PAIR)

        run_of_first = {}
        for r in range(3, len(RUNS)):
            run_of_first[RUNS[r][0]] = r

        transpose_a()
        mix(0)
        mix(1)
        quantise_agg(0)
        spread(0, "g", m_all, nc.vector.tensor_copy)
        g_ps0 = product_g(0)
        quantise_agg(1)
        scaled0 = scale_g(g_ps0, 1)
        g_ps1 = product_g(1)
        scaled1 = scale_g(g_ps1, 1)
        copy_run(0, transpose_run(0), nc.scalar.copy)
        quantise_run(0)
        copy_run(1, transpose_run(1), nc.vector.tensor_copy)
        quantise_run(1)
        spread(1, "o", b_all, nc.scalar.copy)
        copy_run(2, transpose_run(2), nc.scalar.copy)
        o_ps0 = product_o(0)
        mix(2)
        o_ps1 = product_o(1)
        mix(3)
        biased0 = add_bias(o_ps0)
        quantise_run(2)
        finish(0, biased0, scaled0, nc.gpsimd, 1)
        biased1 = add_bias(o_ps1)
        quantise_agg(2)
        quantise_agg(3)
        finish(1, biased1, scaled1, nc.gpsimd, 1)

        for s in range(2, SAMPLES):
            fronts = []
            for b in range(4, SAMPLES):
                if front_step(b) == s:
                    fronts.append(b)
            due = []
            for b in fronts:
                if b in run_of_first:
                    copy_run(run_of_first[b], transpose_run(run_of_first[b]), nc.scalar.copy)
            o_ps = product_o(s)
            early = fronts[:1] if s < FILL else []
            for b in early:
                mix(b)
            g_ps = product_g(s)
            for b in fronts[len(early) :]:
                mix(b)
            for b in fronts:
                if b in run_of_first:
                    due.append(run_of_first[b])
            last = s == SAMPLES - 1
            biased = add_bias(o_ps)
            scaled = scale_g(g_ps, 2 if last else 1)
            for b in range(4, SAMPLES):
                if max(b - 2, front_step(b)) == s:
                    quantise_agg(b)
            for r in due:
                quantise_run(r)
            if last:
                finish(s, biased, scaled, nc.vector, 2)
            else:
                finish(s, biased, scaled, nc.gpsimd, 1)
